import numpy as np
import ml_dtypes


def mxq(x, axis, fmt="e4m3"):
    dtype, down = {"e4m3": (ml_dtypes.float8_e4m3fn, 7), "e5m2": (ml_dtypes.float8_e5m2, 14)}[fmt]
    v = np.moveaxis(np.asarray(x, np.float32).astype(ml_dtypes.bfloat16).astype(np.float64), axis, -1)
    blocks = v.reshape(v.shape[:-1] + (-1, 32))
    amax = np.abs(blocks).max(-1, keepdims=True)
    byte = np.maximum(np.where(amax > 0, np.frexp(amax)[1] - 1 + 127, 0) - down, 1)
    scale = np.exp2(byte - 127.0)
    codes = (blocks / scale).astype(np.float32).astype(dtype).astype(np.float64)
    return np.moveaxis((codes * scale).reshape(v.shape), -1, axis)


WIDE = False


def mx_kscale(k):
    if not WIDE:
        return np.ones(k)
    levels = np.array([10, -10, 5, -5, 0])
    a = np.random.permutation(np.resize(levels, k // 512 * 4)).reshape(k // 512, 4)
    idx = np.arange(k)
    return np.exp2(a[idx // 512, idx % 128 // 32])


BF16 = ml_dtypes.bfloat16


def bf(x):
    return np.asarray(x, np.float32).astype(BF16)


def f64(x):
    return np.asarray(x).astype(np.float64)


E2M1 = np.array([0.0, 0.5, 1.0, 1.5, 2.0, 3.0, 4.0, 6.0, -0.0, -0.5, -1.0, -1.5, -2.0, -3.0, -4.0, -6.0])


def pack_weight(w, fmt):
    k, n = w.shape
    w = f64(bf(w)).reshape(k // 32, 32, n)
    amax = np.abs(w).max(1)
    if fmt == "e4m3":
        byte = np.frexp(amax)[1] - 1 + 127 - 7
    else:
        mant, ex = np.frexp(amax / 6.0)
        byte = np.where(mant > 0.5, ex, ex - 1) + 127
    byte = np.clip(np.where(amax > 0, byte, 1), 1, 254)
    scaled = (w * np.exp2(127.0 - byte)[:, None, :]).reshape(k, n).astype(np.float32)
    by_word = np.ascontiguousarray(scaled.reshape(k // 512, 128, 4, n).transpose(0, 1, 3, 2))
    if fmt == "e4m3":
        words = by_word.astype(ml_dtypes.float8_e4m3fn).view(np.uint8)
    else:
        c = by_word.astype(ml_dtypes.float4_e2m1fn).view(np.uint8) & 0xF
        words = c[..., 0::2] | (c[..., 1::2] << 4)
    return np.ascontiguousarray(words), np.ascontiguousarray(byte.astype(np.uint8).reshape(k // 512, 16, n))


def unpack_weight(words, scales, fmt):
    g, p, n, _ = words.shape
    if fmt == "e4m3":
        vals = np.ascontiguousarray(words).view(ml_dtypes.float8_e4m3fn).astype(np.float64)
    else:
        nib = np.empty((g, p, n, 4), np.uint8)
        nib[..., 0::2] = words & 0xF
        nib[..., 1::2] = words >> 4
        vals = E2M1[nib]
    vals = vals * np.repeat(np.exp2(scales.astype(np.float64) - 127.0), 8, axis=1)[..., None]
    return vals.transpose(0, 1, 3, 2).reshape(g * 512, n)


N, LQ, LK, DIN, D, H = 16, 8, 8, 2048, 2048, 8
DH = D // H


def setup_inputs():
    s, t = mx_kscale(DIN), mx_kscale(D)
    c = D ** -0.25
    mask = (np.random.random((N, LQ)) < 0.75).astype(np.float64)
    mask[:, 0] = 1.0
    query_states = bf(np.random.standard_normal((N, LQ, DIN)) * s)
    key_states = bf(np.random.standard_normal((N, LK, DIN)) * s)
    wq = np.random.standard_normal((D, DIN)) * c / np.sqrt(DIN) / s[None, :] * t[:, None]
    Wq_words, Wq_scales = pack_weight(np.ascontiguousarray(wq.T), "e4m3")
    bq = bf(np.random.standard_normal(D) * 0.5 * c * t)
    wk = np.random.standard_normal((D, DIN)) * c / np.sqrt(DIN) / s[None, :] / t[:, None]
    Wk_words, Wk_scales = pack_weight(np.ascontiguousarray(wk.T), "e4m3")
    bk = bf(np.random.standard_normal(D) * 0.5 * c / t)
    logit_scale = bf(np.random.standard_normal(1) * 0.1)
    return {"query_states": query_states,
            "key_states": key_states,
            "attention_mask": bf(mask),
            "Wq_words": Wq_words,
            "Wq_scales": Wq_scales,
            "bq": bq,
            "Wk_words": Wk_words,
            "Wk_scales": Wk_scales,
            "bk": bk,
            "logit_scale": logit_scale}


def reference(query_states, key_states, attention_mask, Wq_words, Wq_scales, bq, Wk_words, Wk_scales, bk, logit_scale):
    n, Lk = key_states.shape[0], key_states.shape[1]
    Lq = query_states.shape[1]
    q = (mxq(f64(query_states), 2, "e4m3") @ unpack_weight(Wq_words, Wq_scales, "e4m3")) + f64(bq)
    k = (mxq(f64(key_states), 2, "e4m3") @ unpack_weight(Wk_words, Wk_scales, "e4m3")) + f64(bk)
    q = q.reshape(n, Lq, H, DH).transpose(0, 2, 1, 3)
    k = k.reshape(n, Lk, H, DH).transpose(0, 2, 1, 3)
    qf = q.transpose(0, 2, 1, 3).reshape(n * Lq, H * DH)
    kf = k.transpose(0, 2, 1, 3).reshape(n * Lk, H * DH)
    logits = (mxq(qf, 1, "e4m3") @ mxq(kf, 1, "e4m3").T).reshape(n, Lq, n, Lk).transpose(0, 2, 1, 3)
    t2v = logits.max(axis=-1)
    v2t = logits.max(axis=-2)
    mask_sum = np.full((n,), float(Lk))
    com_mask_sum = f64(attention_mask).sum(-1)
    t2v = t2v.sum(axis=2) / com_mask_sum[:, None]
    v2t = v2t.sum(axis=2) / mask_sum[None, :]
    r = (t2v + v2t) / 2.0
    r = np.exp(f64(logit_scale)) * r
    return (r, r.T)

@@ -1,0 +1,218 @@
+from contextlib import ExitStack
+
+import concourse.mybir as mybir
+from concourse.masks import make_identity
+
+F32 = mybir.dt.float32
+BF16 = mybir.dt.bfloat16
+I32 = mybir.dt.int32
+U32 = mybir.dt.uint32
+U8 = mybir.dt.uint8
+FP8X4 = mybir.dt.float8_e4m3fn_x4
+ALU = mybir.AluOpType
+ACT = mybir.ActivationFunctionType
+AX = mybir.AxisListType
+
+P = 128
+DIN = 2048
+D = 2048
+NSEQ = 16
+LTOK = 8
+KG = DIN // 512
+FG = D // 512
+FLOPS = 2 * 2 * P * DIN * D + 2 * P * P * D
+
+CUTS = {"q": ((0, 1024), (1024, 2048)), "k": ((0, 1024), (1024, 1536), (1536, 2048))}
+
+
+def tile_contraattention_w_kernel(
+    tc,
+    query_states,
+    key_states,
+    attention_mask,
+    Wq_words,
+    Wq_scales,
+    bq,
+    Wk_words,
+    Wk_scales,
+    bk,
+    logit_scale,
+    out_0,
+    out_1,
+):
+    nc = tc.nc
+    sides = ("q", "k")
+    x_dram = {"q": query_states, "k": key_states}
+    w_dram = {"q": Wq_words, "k": Wk_words}
+    s_dram = {"q": Wq_scales, "k": Wk_scales}
+    b_dram = {"q": bq, "k": bk}
+    with ExitStack() as ctx:
+        keep = ctx.enter_context(tc.tile_pool(name="keep", bufs=1))
+        psw = ctx.enter_context(tc.psum_pool(name="psw", bufs=4))
+        psk = ctx.enter_context(tc.psum_pool(name="psk", bufs=1))
+        ctx.enter_context(tc.manual_schedule())
+
+        planes = keep.tile([P, 2, D], U8, name="planes", align_bytes=64)
+        nc.vector.memset(planes[:].rearrange("p w n -> p (w n)").bitcast(I32), 0)
+
+        x_sb = {}
+        for s in sides:
+            x_sb[s] = keep.tile([P, DIN], BF16, name="x_" + s)
+            nc.sync.dma_start(out=x_sb[s][:], in_=x_dram[s].rearrange("a l d -> (a l) d"))
+        for wi, s in enumerate(sides):
+            for quad in range(4):
+                nc.sync.dma_start(
+                    out=planes[32 * quad : 32 * quad + 16, wi, :].bitcast(I32),
+                    in_=s_dram[s][:, 4 * quad : 4 * quad + 4, :].bitcast(I32),
+                )
+        w_sb = {}
+        for s in sides:
+            view = w_dram[s].rearrange("g p n t -> p g (n t)").bitcast(I32)
+            for n0, n1 in CUTS[s]:
+                wt = keep.tile([P, KG, n1 - n0], U32, name="w_%s_%d" % (s, n0), align_bytes=64)
+                nc.sync.dma_start(out=wt[:].bitcast(I32), in_=view[:, :, n0:n1])
+                for c in range(n0 // P, n1 // P):
+                    w_sb[(s, c)] = (wt, c * P - n0)
+
+        ident = keep.tile([P, P], F32, name="ident")
+        make_identity(nc, ident[:])
+        bstage = keep.tile([P, P], BF16, name="bstage")
+        nc.gpsimd.memset(bstage[:], 0.0)
+        t1 = keep.tile([P, P], F32, name="t1")
+        nc.gpsimd.memset(t1[:], 0.0)
+        t2 = keep.tile([P, P], F32, name="t2")
+        nc.gpsimd.memset(t2[:], 0.0)
+
+        for wi, s in enumerate(sides):
+            nc.scalar.dma_start(
+                out=bstage[16 * wi : 16 * wi + 16, :], in_=b_dram[s].rearrange("(c p) -> c p", p=P)
+            )
+        m8 = keep.tile([P, LTOK], BF16, name="m8")
+        nc.scalar.dma_start(out=m8[:], in_=attention_mask.unsqueeze(1).to_broadcast([NSEQ, LTOK, LTOK]))
+        ls = keep.tile([P, 1], BF16, name="ls")
+        nc.scalar.dma_start(out=ls[:], in_=logit_scale.partition_broadcast(P))
+
+        ident_bf = keep.tile([P, P], BF16, name="ident_bf")
+        nc.vector.tensor_copy(out=ident_bf[:], in_=ident[:])
+        blk = keep.tile([P, NSEQ], F32, name="blk")
+        nc.vector.tensor_reduce(
+            out=blk[:], in_=ident[:].rearrange("p (a l) -> p a l", l=LTOK), axis=AX.X, op=ALU.add
+        )
+
+        xc = {}
+        xp = {}
+        for s in sides:
+            xw = x_sb[s][:].bitcast(F32)
+            xg = keep.tile([P, KG, P, 4], BF16, name="xg_" + s, align_bytes=64)
+            xgw = xg[:].bitcast(F32)
+            for h in range(2):
+                xt = psw.tile([P, 2, 2, P], F32, name="xt_%s_%d" % (s, h), tag="work")
+                for gl in range(2):
+                    g = 2 * h + gl
+                    for u in range(2):
+                        nc.tensor.transpose(xt[:, gl, u, :], xw[:, 256 * g + u : 256 * (g + 1) : 2], ident[:])
+                src = xt[:].rearrange("p g u w -> p g w u")
+                dst = xgw[:, 2 * h : 2 * h + 2, :, :]
+                if h == 0:
+                    nc.vector.tensor_copy(out=dst, in_=src)
+                else:
+                    nc.scalar.copy(out=dst, in_=src)
+            xc[s] = keep.tile([P, KG * P], U32, name="xc_" + s, align_bytes=64)
+            xp[s] = keep.tile([P, KG * P], U8, name="xp_" + s, align_bytes=64)
+            nc.vector.quantize_mx(
+                out=xc[s][:].bitcast(FP8X4), scales=xp[s][:], in_=xg[:].rearrange("p g w t -> p (g w t)")
+            )
+
+        bt = psk.tile([P, P], BF16, name="bt")
+        nc.tensor.transpose(bt[:], bstage[:], ident_bf[:])
+        bias = keep.tile([P, 32], F32, name="bias")
+        nc.vector.tensor_copy(out=bias[:], in_=bt[:, 0:32])
+
+        els = keep.tile([P, 1], F32, name="els")
+        nc.scalar.activation(out=els[:], in_=ls[:], func=ACT.Exp)
+        msum = keep.tile([P, 1], F32, name="msum")
+        nc.vector.tensor_reduce(out=msum[:], in_=m8[:], axis=AX.X, op=ALU.add)
+        rec = keep.tile([P, 1], F32, name="rec")
+        nc.vector.reciprocal(out=rec[:], in_=msum[:])
+        w1 = keep.tile([P, 1], F32, name="w1")
+        nc.vector.tensor_scalar(out=w1[:], in0=rec[:], scalar1=els[:, 0:1], scalar2=0.5, op0=ALU.mult, op1=ALU.mult)
+        nc.vector.tensor_scalar(out=t1[:, 32:48], in0=blk[:], scalar1=w1[:, 0:1], scalar2=None, op0=ALU.mult)
+        nc.vector.tensor_scalar(
+            out=t2[:, 0:16], in0=blk[:], scalar1=els[:, 0:1], scalar2=0.5 / LTOK, op0=ALU.mult, op1=ALU.mult
+        )
+
+        fg = {}
+        fc = {}
+        fp = {}
+        for s in sides:
+            fg[s] = keep.tile([P, FG, P, 4], BF16, name="fg_" + s, align_bytes=64)
+            fc[s] = keep.tile([P, FG * P], U32, name="fc_" + s, align_bytes=64)
+            fp[s] = keep.tile([P, FG * P], U8, name="fp_" + s, align_bytes=64)
+
+        def project(s, grp):
+            wi = sides.index(s)
+            ps = psw.tile([P, 4, P], F32, name="ps_%s_%d" % (s, grp), tag="work")
+            for t in range(4):
+                c = 4 * grp + t
+                wt, col = w_sb[(s, c)]
+                for g in range(KG):
+                    nc.tensor.matmul_mx(
+                        out=ps[:, t, :],
+                        lhsT=wt[:, g, col : col + P].bitcast(FP8X4),
+                        lhsT_scale=planes[4 * g : P, wi, c * P : (c + 1) * P],
+                        rhs=xc[s][:, g * P : (g + 1) * P].bitcast(FP8X4),
+                        rhs_scale=xp[s][:, g * P : (g + 1) * P],
+                        start=(g == 0),
+                        stop=(g == KG - 1),
+                    )
+            b0 = 16 * wi + 4 * grp
+            nc.vector.tensor_tensor(
+                out=fg[s][:, grp, :, :],
+                in0=ps[:].rearrange("p t w -> p w t"),
+                in1=bias[:, b0 : b0 + 4].unsqueeze(1).to_broadcast([P, P, 4]),
+                op=ALU.add,
+            )
+            cols = slice(grp * P, (grp + 1) * P)
+            nc.vector.quantize_mx(
+                out=fc[s][:, cols].bitcast(FP8X4),
+                scales=fp[s][:, cols],
+                in_=fg[s][:, grp, :, :].rearrange("p w t -> p (w t)"),
+            )
+
+        lg = psk.tile([P, P], F32, name="lg")
+        lgt = psk.tile([P, P], F32, name="lgt")
+
+        def logits(grp):
+            cols = slice(grp * P, (grp + 1) * P)
+            for acc, a, b in ((lg, "q", "k"), (lgt, "k", "q")):
+                nc.tensor.matmul_mx(
+                    out=acc[:],
+                    lhsT=fc[a][:, cols].bitcast(FP8X4),
+                    lhsT_scale=fp[a][:, cols],
+                    rhs=fc[b][:, cols].bitcast(FP8X4),
+                    rhs_scale=fp[b][:, cols],
+                    start=(grp == 0),
+                    stop=(grp == FG - 1),
+                )
+
+        for grp in range(FG):
+            project("q", grp)
+        for grp in range(FG):
+            project("k", grp)
+            if grp > 0:
+                logits(grp - 1)
+        logits(FG - 1)
+
+        nc.vector.tensor_reduce(
+            out=t1[:, 0:16], in_=lg[:].rearrange("p (b m) -> p b m", m=LTOK), axis=AX.X, op=ALU.max
+        )
+        nc.vector.tensor_reduce(
+            out=t2[:, 32:48], in_=lgt[:].rearrange("p (a l) -> p a l", l=LTOK), axis=AX.X, op=ALU.max
+        )
+        fin = psk.tile([P, 48], F32, name="fin")
+        nc.tensor.matmul(out=fin[:], lhsT=t1[:], rhs=t1[:, 0:48], start=True, stop=False)
+        nc.tensor.matmul(out=fin[:], lhsT=t2[:], rhs=t2[:, 0:48], start=False, stop=True)
+        res = keep.tile([P, 48], F32, name="res")
+        nc.vector.tensor_copy(out=res[:], in_=fin[:])
+        nc.sync.dma_start(out=out_0, in_=res[32:48, 0:16])
+        nc.sync.dma_start(out=out_1, in_=res[0:16, 32:48])

@@ -22,7 +22,8 @@ KG = DIN // 512
 FG = D // 512
 FLOPS = 2 * 2 * P * DIN * D + 2 * P * P * D
 
-CUTS = {"q": ((0, 1024), (1024, 2048)), "k": ((0, 1024), (1024, 1536), (1536, 2048))}
+CUTS = {"q": ((0, 1024), (1024, 2048)), "k": ((0, 512), (512, 1024), (1024, 1536))}
+LAST0 = 1536
 
 
 def tile_contraattention_w_kernel(
@@ -59,38 +60,45 @@ def tile_contraattention_w_kernel(
         for s in sides:
             x_sb[s] = keep.tile([P, DIN], BF16, name="x_" + s)
             nc.sync.dma_start(out=x_sb[s][:], in_=x_dram[s].rearrange("a l d -> (a l) d"))
-        for wi, s in enumerate(sides):
-            for quad in range(4):
-                nc.sync.dma_start(
-                    out=planes[32 * quad : 32 * quad + 16, wi, :].bitcast(I32),
-                    in_=s_dram[s][:, 4 * quad : 4 * quad + 4, :].bitcast(I32),
-                )
-        w_sb = {}
-        for s in sides:
-            view = w_dram[s].rearrange("g p n t -> p g (n t)").bitcast(I32)
-            for n0, n1 in CUTS[s]:
-                wt = keep.tile([P, KG, n1 - n0], U32, name="w_%s_%d" % (s, n0), align_bytes=64)
-                nc.sync.dma_start(out=wt[:].bitcast(I32), in_=view[:, :, n0:n1])
-                for c in range(n0 // P, n1 // P):
-                    w_sb[(s, c)] = (wt, c * P - n0)
-
         ident = keep.tile([P, P], F32, name="ident")
-        make_identity(nc, ident[:])
         bstage = keep.tile([P, P], BF16, name="bstage")
         nc.gpsimd.memset(bstage[:], 0.0)
+        make_identity(nc, ident[:])
         t1 = keep.tile([P, P], F32, name="t1")
         nc.gpsimd.memset(t1[:], 0.0)
         t2 = keep.tile([P, P], F32, name="t2")
         nc.gpsimd.memset(t2[:], 0.0)
 
+        w_sb = {}
+
+        def load_scales(s):
+            wi = sides.index(s)
+            for quad in range(4):
+                nc.sync.dma_start(
+                    out=planes[32 * quad : 32 * quad + 16, wi, :].bitcast(I32),
+                    in_=s_dram[s][:, 4 * quad : 4 * quad + 4, :].bitcast(I32),
+                )
+
+        def load_words(s, n0, n1, g0, g1):
+            view = w_dram[s].rearrange("g p n t -> p g (n t)").bitcast(I32)
+            wt = keep.tile([P, g1 - g0, n1 - n0], U32, name="w_%s_%d_%d" % (s, n0, g0), align_bytes=64)
+            nc.sync.dma_start(out=wt[:].bitcast(I32), in_=view[:, g0:g1, n0:n1])
+            for c in range(n0 // P, n1 // P):
+                for g in range(g0, g1):
+                    w_sb[(s, c, g)] = wt[:, g - g0, c * P - n0 : (c + 1) * P - n0]
+
+        load_scales("q")
+        for n0, n1 in CUTS["q"]:
+            load_words("q", n0, n1, 0, KG)
         for wi, s in enumerate(sides):
             nc.scalar.dma_start(
                 out=bstage[16 * wi : 16 * wi + 16, :], in_=b_dram[s].rearrange("(c p) -> c p", p=P)
             )
-        m8 = keep.tile([P, LTOK], BF16, name="m8")
-        nc.scalar.dma_start(out=m8[:], in_=attention_mask.unsqueeze(1).to_broadcast([NSEQ, LTOK, LTOK]))
-        ls = keep.tile([P, 1], BF16, name="ls")
-        nc.scalar.dma_start(out=ls[:], in_=logit_scale.partition_broadcast(P))
+        load_scales("k")
+        for n0, n1 in CUTS["k"]:
+            load_words("k", n0, n1, 0, KG)
+        load_words("k", LAST0, D, 0, KG - 1)
+        load_words("k", LAST0, D, KG - 1, KG)
 
         ident_bf = keep.tile([P, P], BF16, name="ident_bf")
         nc.vector.tensor_copy(out=ident_bf[:], in_=ident[:])
@@ -128,18 +136,26 @@ def tile_contraattention_w_kernel(
         bias = keep.tile([P, 32], F32, name="bias")
         nc.vector.tensor_copy(out=bias[:], in_=bt[:, 0:32])
 
+        m8 = keep.tile([P, LTOK], BF16, name="m8")
+        nc.scalar.dma_start(out=m8[:], in_=attention_mask.unsqueeze(1).to_broadcast([NSEQ, LTOK, LTOK]))
+        ls = keep.tile([P, 1], BF16, name="ls")
+        nc.scalar.dma_start(out=ls[:], in_=logit_scale.partition_broadcast(P))
         els = keep.tile([P, 1], F32, name="els")
         nc.scalar.activation(out=els[:], in_=ls[:], func=ACT.Exp)
-        msum = keep.tile([P, 1], F32, name="msum")
-        nc.vector.tensor_reduce(out=msum[:], in_=m8[:], axis=AX.X, op=ALU.add)
-        rec = keep.tile([P, 1], F32, name="rec")
-        nc.vector.reciprocal(out=rec[:], in_=msum[:])
-        w1 = keep.tile([P, 1], F32, name="w1")
-        nc.vector.tensor_scalar(out=w1[:], in0=rec[:], scalar1=els[:, 0:1], scalar2=0.5, op0=ALU.mult, op1=ALU.mult)
-        nc.vector.tensor_scalar(out=t1[:, 32:48], in0=blk[:], scalar1=w1[:, 0:1], scalar2=None, op0=ALU.mult)
-        nc.vector.tensor_scalar(
-            out=t2[:, 0:16], in0=blk[:], scalar1=els[:, 0:1], scalar2=0.5 / LTOK, op0=ALU.mult, op1=ALU.mult
-        )
+
+        def sum_weights():
+            msum = keep.tile([P, 1], F32, name="msum")
+            nc.vector.tensor_reduce(out=msum[:], in_=m8[:], axis=AX.X, op=ALU.add)
+            rec = keep.tile([P, 1], F32, name="rec")
+            nc.vector.reciprocal(out=rec[:], in_=msum[:])
+            w1 = keep.tile([P, 1], F32, name="w1")
+            nc.vector.tensor_scalar(
+                out=w1[:], in0=rec[:], scalar1=els[:, 0:1], scalar2=0.5, op0=ALU.mult, op1=ALU.mult
+            )
+            nc.vector.tensor_scalar(out=t1[:, 32:48], in0=blk[:], scalar1=w1[:, 0:1], scalar2=None, op0=ALU.mult)
+            nc.vector.tensor_scalar(
+                out=t2[:, 0:16], in0=blk[:], scalar1=els[:, 0:1], scalar2=0.5 / LTOK, op0=ALU.mult, op1=ALU.mult
+            )
 
         fg = {}
         fc = {}
@@ -149,35 +165,39 @@ def tile_contraattention_w_kernel(
             fc[s] = keep.tile([P, FG * P], U32, name="fc_" + s, align_bytes=64)
             fp[s] = keep.tile([P, FG * P], U8, name="fp_" + s, align_bytes=64)
 
-        def project(s, grp):
+        def passes(s, grp, g0, g1, label):
             wi = sides.index(s)
-            ps = psw.tile([P, 4, P], F32, name="ps_%s_%d" % (s, grp), tag="work")
+            ps = psw.tile([P, 4, P], F32, name="ps_%s_%d_%s" % (s, grp, label), tag="work")
             for t in range(4):
                 c = 4 * grp + t
-                wt, col = w_sb[(s, c)]
-                for g in range(KG):
+                for g in range(g0, g1):
                     nc.tensor.matmul_mx(
                         out=ps[:, t, :],
-                        lhsT=wt[:, g, col : col + P].bitcast(FP8X4),
+                        lhsT=w_sb[(s, c, g)].bitcast(FP8X4),
                         lhsT_scale=planes[4 * g : P, wi, c * P : (c + 1) * P],
                         rhs=xc[s][:, g * P : (g + 1) * P].bitcast(FP8X4),
                         rhs_scale=xp[s][:, g * P : (g + 1) * P],
-                        start=(g == 0),
-                        stop=(g == KG - 1),
+                        start=(g == g0),
+                        stop=(g == g1 - 1),
                     )
-            b0 = 16 * wi + 4 * grp
-            nc.vector.tensor_tensor(
-                out=fg[s][:, grp, :, :],
-                in0=ps[:].rearrange("p t w -> p w t"),
-                in1=bias[:, b0 : b0 + 4].unsqueeze(1).to_broadcast([P, P, 4]),
-                op=ALU.add,
-            )
+            return ps[:].rearrange("p t w -> p w t")
+
+        def bias_of(s, grp):
+            b0 = 16 * sides.index(s) + 4 * grp
+            return bias[:, b0 : b0 + 4].unsqueeze(1).to_broadcast([P, P, 4])
+
+        def quantise(s, grp):
             cols = slice(grp * P, (grp + 1) * P)
             nc.vector.quantize_mx(
                 out=fc[s][:, cols].bitcast(FP8X4),
                 scales=fp[s][:, cols],
                 in_=fg[s][:, grp, :, :].rearrange("p w t -> p (w t)"),
             )
+
+        def project(s, grp):
+            sums = passes(s, grp, 0, KG, "all")
+            nc.vector.tensor_tensor(out=fg[s][:, grp, :, :], in0=sums, in1=bias_of(s, grp), op=ALU.add)
+            quantise(s, grp)
 
         lg = psk.tile([P, P], F32, name="lg")
         lgt = psk.tile([P, P], F32, name="lgt")
@@ -197,11 +217,21 @@ def tile_contraattention_w_kernel(
 
         for grp in range(FG):
             project("q", grp)
-        for grp in range(FG):
+        last = FG - 1
+        for grp in range(last):
             project("k", grp)
-            if grp > 0:
+            if grp == 0:
+                sum_weights()
+            else:
                 logits(grp - 1)
-        logits(FG - 1)
+        early = passes("k", last, 0, KG - 1, "early")
+        part = keep.tile([P, P, 4], F32, name="part")
+        nc.vector.tensor_tensor(out=part[:], in0=early, in1=bias_of("k", last), op=ALU.add)
+        logits(last - 1)
+        late = passes("k", last, KG - 1, KG, "late")
+        nc.vector.tensor_tensor(out=fg["k"][:, last, :, :], in0=late, in1=part[:], op=ALU.add)
+        quantise("k", last)
+        logits(last)
 
         nc.vector.tensor_reduce(
             out=t1[:, 0:16], in_=lg[:].rearrange("p (b m) -> p b m", m=LTOK), axis=AX.X, op=ALU.max

@@ -22,8 +22,21 @@ KG = DIN // 512
 FG = D // 512
 FLOPS = 2 * 2 * P * DIN * D + 2 * P * P * D
 
-CUTS = {"q": ((0, 1024), (1024, 2048)), "k": ((0, 512), (512, 1024), (1024, 1536))}
-LAST0 = 1536
+PIECES = (
+    ("q", 0, 2048, 0, 1),
+    ("q", 0, 2048, 1, 2),
+    ("q", 0, 2048, 2, 3),
+    ("q", 0, 2048, 3, 4),
+    ("k", 0, 1024, 0, 1),
+    ("k", 0, 1024, 1, 2),
+    ("k", 0, 1024, 2, 3),
+    ("k", 0, 1024, 3, 4),
+    ("k", 1024, 2048, 0, 1),
+    ("k", 1024, 2048, 1, 2),
+    ("k", 1024, 1536, 2, 4),
+    ("k", 1536, 2048, 2, 3),
+    ("k", 1536, 2048, 3, 4),
+)
 
 
 def tile_contraattention_w_kernel(
@@ -64,10 +77,10 @@ def tile_contraattention_w_kernel(
         bstage = keep.tile([P, P], BF16, name="bstage")
         nc.gpsimd.memset(bstage[:], 0.0)
         make_identity(nc, ident[:])
-        t1 = keep.tile([P, P], F32, name="t1")
-        nc.gpsimd.memset(t1[:], 0.0)
-        t2 = keep.tile([P, P], F32, name="t2")
-        nc.gpsimd.memset(t2[:], 0.0)
+        gram = {}
+        for nm in ("1h", "1l", "2h", "2l"):
+            gram[nm] = keep.tile([P, P], BF16, name="gram_" + nm)
+            nc.gpsimd.memset(gram[nm][:], 0.0)
 
         w_sb = {}
 
@@ -88,17 +101,15 @@ def tile_contraattention_w_kernel(
                     w_sb[(s, c, g)] = wt[:, g - g0, c * P - n0 : (c + 1) * P - n0]
 
         load_scales("q")
-        for n0, n1 in CUTS["q"]:
-            load_words("q", n0, n1, 0, KG)
-        for wi, s in enumerate(sides):
-            nc.scalar.dma_start(
-                out=bstage[16 * wi : 16 * wi + 16, :], in_=b_dram[s].rearrange("(c p) -> c p", p=P)
-            )
-        load_scales("k")
-        for n0, n1 in CUTS["k"]:
-            load_words("k", n0, n1, 0, KG)
-        load_words("k", LAST0, D, 0, KG - 1)
-        load_words("k", LAST0, D, KG - 1, KG)
+        for i, piece in enumerate(PIECES):
+            if i == 2:
+                for wi, s in enumerate(sides):
+                    nc.scalar.dma_start(
+                        out=bstage[16 * wi : 16 * wi + 16, :], in_=b_dram[s].rearrange("(c p) -> c p", p=P)
+                    )
+            if i == 4:
+                load_scales("k")
+            load_words(*piece)
 
         ident_bf = keep.tile([P, P], BF16, name="ident_bf")
         nc.vector.tensor_copy(out=ident_bf[:], in_=ident[:])
@@ -143,19 +154,22 @@ def tile_contraattention_w_kernel(
         els = keep.tile([P, 1], F32, name="els")
         nc.scalar.activation(out=els[:], in_=ls[:], func=ACT.Exp)
 
+        w1 = keep.tile([P, 1], F32, name="w1")
+        w2 = keep.tile([P, 1], F32, name="w2")
+
         def sum_weights():
             msum = keep.tile([P, 1], F32, name="msum")
             nc.vector.tensor_reduce(out=msum[:], in_=m8[:], axis=AX.X, op=ALU.add)
             rec = keep.tile([P, 1], F32, name="rec")
             nc.vector.reciprocal(out=rec[:], in_=msum[:])
-            w1 = keep.tile([P, 1], F32, name="w1")
             nc.vector.tensor_scalar(
                 out=w1[:], in0=rec[:], scalar1=els[:, 0:1], scalar2=0.5, op0=ALU.mult, op1=ALU.mult
             )
-            nc.vector.tensor_scalar(out=t1[:, 32:48], in0=blk[:], scalar1=w1[:, 0:1], scalar2=None, op0=ALU.mult)
-            nc.vector.tensor_scalar(
-                out=t2[:, 0:16], in0=blk[:], scalar1=els[:, 0:1], scalar2=0.5 / LTOK, op0=ALU.mult, op1=ALU.mult
-            )
+            nc.vector.tensor_scalar(out=w2[:], in0=els[:], scalar1=0.5 / LTOK, scalar2=None, op0=ALU.mult)
+            for nm in ("1h", "1l"):
+                nc.vector.tensor_copy(out=gram[nm][:, 32:48], in_=blk[:])
+            for nm in ("2h", "2l"):
+                nc.vector.tensor_copy(out=gram[nm][:, 0:16], in_=blk[:])
 
         fg = {}
         fc = {}
@@ -165,22 +179,27 @@ def tile_contraattention_w_kernel(
             fc[s] = keep.tile([P, FG * P], U32, name="fc_" + s, align_bytes=64)
             fp[s] = keep.tile([P, FG * P], U8, name="fp_" + s, align_bytes=64)
 
-        def passes(s, grp, g0, g1, label):
+        banks = {}
+        done = {}
+
+        def passes(s, n0, n1, g0, g1):
             wi = sides.index(s)
-            ps = psw.tile([P, 4, P], F32, name="ps_%s_%d_%s" % (s, grp, label), tag="work")
-            for t in range(4):
-                c = 4 * grp + t
-                for g in range(g0, g1):
+            for g in range(g0, g1):
+                for c in range(n0 // P, n1 // P):
+                    grp = c // 4
+                    if (s, grp) not in banks:
+                        banks[(s, grp)] = psw.tile([P, 4, P], F32, name="ps_%s_%d" % (s, grp), tag="work")
+                        done[(s, grp)] = 0
                     nc.tensor.matmul_mx(
-                        out=ps[:, t, :],
+                        out=banks[(s, grp)][:, c % 4, :],
                         lhsT=w_sb[(s, c, g)].bitcast(FP8X4),
                         lhsT_scale=planes[4 * g : P, wi, c * P : (c + 1) * P],
                         rhs=xc[s][:, g * P : (g + 1) * P].bitcast(FP8X4),
                         rhs_scale=xp[s][:, g * P : (g + 1) * P],
-                        start=(g == g0),
-                        stop=(g == g1 - 1),
+                        start=(done[(s, grp)] == 0),
+                        stop=(done[(s, grp)] == 4 * KG - 1),
                     )
-            return ps[:].rearrange("p t w -> p w t")
+                    done[(s, grp)] = done[(s, grp)] + 1
 
         def bias_of(s, grp):
             b0 = 16 * sides.index(s) + 4 * grp
@@ -194,9 +213,13 @@ def tile_contraattention_w_kernel(
                 in_=fg[s][:, grp, :, :].rearrange("p w t -> p (w t)"),
             )
 
-        def project(s, grp):
-            sums = passes(s, grp, 0, KG, "all")
-            nc.vector.tensor_tensor(out=fg[s][:, grp, :, :], in0=sums, in1=bias_of(s, grp), op=ALU.add)
+        def finish(s, grp):
+            nc.vector.tensor_tensor(
+                out=fg[s][:, grp, :, :],
+                in0=banks[(s, grp)][:].rearrange("p t w -> p w t"),
+                in1=bias_of(s, grp),
+                op=ALU.add,
+            )
             quantise(s, grp)
 
         lg = psk.tile([P, P], F32, name="lg")
@@ -215,33 +238,41 @@ def tile_contraattention_w_kernel(
                     stop=(grp == FG - 1),
                 )
 
-        for grp in range(FG):
-            project("q", grp)
-        last = FG - 1
-        for grp in range(last):
-            project("k", grp)
-            if grp == 0:
+        for i, piece in enumerate(PIECES):
+            passes(*piece)
+            if i == 3:
+                for grp in range(FG):
+                    finish("q", grp)
+            if i == 7:
+                finish("k", 0)
+                finish("k", 1)
                 sum_weights()
-            else:
-                logits(grp - 1)
-        early = passes("k", last, 0, KG - 1, "early")
-        part = keep.tile([P, P, 4], F32, name="part")
-        nc.vector.tensor_tensor(out=part[:], in0=early, in1=bias_of("k", last), op=ALU.add)
-        logits(last - 1)
-        late = passes("k", last, KG - 1, KG, "late")
-        nc.vector.tensor_tensor(out=fg["k"][:, last, :, :], in0=late, in1=part[:], op=ALU.add)
-        quantise("k", last)
-        logits(last)
+            if i == 9:
+                logits(0)
+                logits(1)
+            if i == 10:
+                finish("k", 2)
+        finish("k", 3)
+        logits(2)
+        logits(3)
 
-        nc.vector.tensor_reduce(
-            out=t1[:, 0:16], in_=lg[:].rearrange("p (b m) -> p b m", m=LTOK), axis=AX.X, op=ALU.max
+        r1 = keep.tile([P, NSEQ], F32, name="r1")
+        r2 = keep.tile([P, NSEQ], F32, name="r2")
+        nc.vector.tensor_reduce(out=r1[:], in_=lg[:].rearrange("p (b m) -> p b m", m=LTOK), axis=AX.X, op=ALU.max)
+        nc.vector.tensor_reduce(out=r2[:], in_=lgt[:].rearrange("p (a l) -> p a l", l=LTOK), axis=AX.X, op=ALU.max)
+        hi1 = gram["1h"][:, 0:16]
+        hi2 = gram["2h"][:, 32:48]
+        nc.vector.tensor_scalar(out=hi1, in0=r1[:], scalar1=w1[:, 0:1], scalar2=None, op0=ALU.mult)
+        nc.vector.tensor_scalar(out=hi2, in0=r2[:], scalar1=w2[:, 0:1], scalar2=None, op0=ALU.mult)
+        nc.vector.scalar_tensor_tensor(
+            out=gram["1l"][:, 0:16], in0=r1[:], scalar=w1[:, 0:1], in1=hi1, op0=ALU.mult, op1=ALU.subtract
         )
-        nc.vector.tensor_reduce(
-            out=t2[:, 32:48], in_=lgt[:].rearrange("p (a l) -> p a l", l=LTOK), axis=AX.X, op=ALU.max
+        nc.vector.scalar_tensor_tensor(
+            out=gram["2l"][:, 32:48], in0=r2[:], scalar=w2[:, 0:1], in1=hi2, op0=ALU.mult, op1=ALU.subtract
         )
         fin = psk.tile([P, 48], F32, name="fin")
-        nc.tensor.matmul(out=fin[:], lhsT=t1[:], rhs=t1[:, 0:48], start=True, stop=False)
-        nc.tensor.matmul(out=fin[:], lhsT=t2[:], rhs=t2[:, 0:48], start=False, stop=True)
+        for i, nm in enumerate(("1h", "2h", "1l", "2l")):
+            nc.tensor.matmul(out=fin[:], lhsT=gram[nm][:], rhs=gram[nm][:, 0:48], start=(i == 0), stop=(i == 3))
         res = keep.tile([P, 48], F32, name="res")
         nc.vector.tensor_copy(out=res[:], in_=fin[:])
         nc.sync.dma_start(out=out_0, in_=res[32:48, 0:16])

@@ -77,6 +77,9 @@ def tile_contraattention_w_kernel(
         bstage = keep.tile([P, P], BF16, name="bstage")
         nc.gpsimd.memset(bstage[:], 0.0)
         make_identity(nc, ident[:])
+        spread = keep.tile([P, P], BF16, name="spread")
+        nc.gpsimd.memset(spread[:], 0.0)
+        nc.gpsimd.memset(spread[64:65, :], 1.0)
         gram = {}
         for nm in ("1h", "1l", "2h", "2l"):
             gram[nm] = keep.tile([P, P], BF16, name="gram_" + nm)
@@ -107,6 +110,8 @@ def tile_contraattention_w_kernel(
                     nc.scalar.dma_start(
                         out=bstage[16 * wi : 16 * wi + 16, :], in_=b_dram[s].rearrange("(c p) -> c p", p=P)
                     )
+                nc.scalar.dma_start(out=bstage[32:48, 0:LTOK], in_=attention_mask)
+                nc.scalar.dma_start(out=bstage[64:65, LTOK : LTOK + 1], in_=logit_scale.unsqueeze(0))
             if i == 4:
                 load_scales("k")
             load_words(*piece)
@@ -116,6 +121,11 @@ def tile_contraattention_w_kernel(
         blk = keep.tile([P, NSEQ], F32, name="blk")
         nc.vector.tensor_reduce(
             out=blk[:], in_=ident[:].rearrange("p (a l) -> p a l", l=LTOK), axis=AX.X, op=ALU.add
+        )
+
+        nc.vector.tensor_copy(
+            out=spread[32:48, :].rearrange("p (a l) -> p a l", l=LTOK),
+            in_=ident[32:48, 32:48].unsqueeze(2).to_broadcast([NSEQ, NSEQ, LTOK]),
         )
 
         xc = {}
@@ -147,19 +157,17 @@ def tile_contraattention_w_kernel(
         bias = keep.tile([P, 32], F32, name="bias")
         nc.vector.tensor_copy(out=bias[:], in_=bt[:, 0:32])
 
-        m8 = keep.tile([P, LTOK], BF16, name="m8")
-        nc.scalar.dma_start(out=m8[:], in_=attention_mask.unsqueeze(1).to_broadcast([NSEQ, LTOK, LTOK]))
-        ls = keep.tile([P, 1], BF16, name="ls")
-        nc.scalar.dma_start(out=ls[:], in_=logit_scale.partition_broadcast(P))
+        fin = psk.tile([P, 64], F32, name="fin")
+        nc.tensor.matmul(out=fin[:, 48:64], lhsT=spread[:], rhs=bstage[:, 0:16], start=True, stop=True)
         els = keep.tile([P, 1], F32, name="els")
-        nc.scalar.activation(out=els[:], in_=ls[:], func=ACT.Exp)
+        nc.scalar.activation(out=els[:], in_=fin[:, 48 + LTOK : 49 + LTOK], func=ACT.Exp)
 
         w1 = keep.tile([P, 1], F32, name="w1")
         w2 = keep.tile([P, 1], F32, name="w2")
 
         def sum_weights():
             msum = keep.tile([P, 1], F32, name="msum")
-            nc.vector.tensor_reduce(out=msum[:], in_=m8[:], axis=AX.X, op=ALU.add)
+            nc.vector.tensor_reduce(out=msum[:], in_=fin[:, 48 : 48 + LTOK], axis=AX.X, op=ALU.add)
             rec = keep.tile([P, 1], F32, name="rec")
             nc.vector.reciprocal(out=rec[:], in_=msum[:])
             nc.vector.tensor_scalar(
@@ -270,10 +278,9 @@ def tile_contraattention_w_kernel(
         nc.vector.scalar_tensor_tensor(
             out=gram["2l"][:, 32:48], in0=r2[:], scalar=w2[:, 0:1], in1=hi2, op0=ALU.mult, op1=ALU.subtract
         )
-        fin = psk.tile([P, 48], F32, name="fin")
         for i, nm in enumerate(("1h", "2h", "1l", "2l")):
-            nc.tensor.matmul(out=fin[:], lhsT=gram[nm][:], rhs=gram[nm][:, 0:48], start=(i == 0), stop=(i == 3))
+            nc.tensor.matmul(out=fin[:, 0:48], lhsT=gram[nm][:], rhs=gram[nm][:, 0:48], start=(i == 0), stop=(i == 3))
         res = keep.tile([P, 48], F32, name="res")
-        nc.vector.tensor_copy(out=res[:], in_=fin[:])
+        nc.vector.tensor_copy(out=res[:], in_=fin[:, 0:48])
         nc.sync.dma_start(out=out_0, in_=res[32:48, 0:16])
         nc.sync.dma_start(out=out_1, in_=res[0:16, 32:48])

@@ -23,17 +23,17 @@ FG = D // 512
 FLOPS = 2 * 2 * P * DIN * D + 2 * P * P * D
 
 PIECES = (
-    ("q", 0, 2048, 0, 1),
-    ("q", 0, 2048, 1, 2),
-    ("q", 0, 2048, 2, 3),
-    ("q", 0, 2048, 3, 4),
+    ("q", 0, 1024, 0, 2),
+    ("q", 0, 1024, 2, 4),
+    ("q", 1024, 2048, 0, 2),
+    ("q", 1024, 2048, 2, 4),
     ("k", 0, 1024, 0, 1),
     ("k", 0, 1024, 1, 2),
     ("k", 0, 1024, 2, 3),
     ("k", 0, 1024, 3, 4),
-    ("k", 1024, 2048, 0, 1),
-    ("k", 1024, 2048, 1, 2),
+    ("k", 1024, 1536, 0, 2),
     ("k", 1024, 1536, 2, 4),
+    ("k", 1536, 2048, 0, 2),
     ("k", 1536, 2048, 2, 3),
     ("k", 1536, 2048, 3, 4),
 )
@@ -69,13 +69,12 @@ def tile_contraattention_w_kernel(
         planes = keep.tile([P, 2, D], U8, name="planes", align_bytes=64)
         nc.vector.memset(planes[:].rearrange("p w n -> p (w n)").bitcast(I32), 0)
 
-        x_sb = {}
-        for s in sides:
-            x_sb[s] = keep.tile([P, DIN], BF16, name="x_" + s)
-            nc.sync.dma_start(out=x_sb[s][:], in_=x_dram[s].rearrange("a l d -> (a l) d"))
-        ident = keep.tile([P, P], F32, name="ident")
         bstage = keep.tile([P, P], BF16, name="bstage")
         nc.gpsimd.memset(bstage[:], 0.0)
+        for wi, s in enumerate(sides):
+            nc.scalar.dma_start(out=bstage[16 * wi : 16 * wi + 16, :], in_=b_dram[s].rearrange("(c p) -> c p", p=P))
+
+        ident = keep.tile([P, P], F32, name="ident")
         make_identity(nc, ident[:])
         spread = keep.tile([P, P], BF16, name="spread")
         nc.gpsimd.memset(spread[:], 0.0)
@@ -84,8 +83,17 @@ def tile_contraattention_w_kernel(
         for nm in ("1h", "1l", "2h", "2l"):
             gram[nm] = keep.tile([P, P], BF16, name="gram_" + nm)
             nc.gpsimd.memset(gram[nm][:], 0.0)
+        mstage = keep.tile([P, NSEQ], BF16, name="mstage")
+        nc.gpsimd.memset(mstage[:], 0.0)
+        nc.gpsimd.dma_start(out=mstage[32:48, 0:LTOK], in_=attention_mask)
+        nc.gpsimd.dma_start(out=mstage[64:65, LTOK : LTOK + 1], in_=logit_scale.unsqueeze(0))
 
+        x_sb = {}
         w_sb = {}
+
+        def load_x(s):
+            x_sb[s] = keep.tile([P, DIN], BF16, name="x_" + s)
+            nc.sync.dma_start(out=x_sb[s][:], in_=x_dram[s].rearrange("a l d -> (a l) d"))
 
         def load_scales(s):
             wi = sides.index(s)
@@ -103,18 +111,14 @@ def tile_contraattention_w_kernel(
                 for g in range(g0, g1):
                     w_sb[(s, c, g)] = wt[:, g - g0, c * P - n0 : (c + 1) * P - n0]
 
-        load_scales("q")
+        load_x("q")
         for i, piece in enumerate(PIECES):
-            if i == 2:
-                for wi, s in enumerate(sides):
-                    nc.scalar.dma_start(
-                        out=bstage[16 * wi : 16 * wi + 16, :], in_=b_dram[s].rearrange("(c p) -> c p", p=P)
-                    )
-                nc.scalar.dma_start(out=bstage[32:48, 0:LTOK], in_=attention_mask)
-                nc.scalar.dma_start(out=bstage[64:65, LTOK : LTOK + 1], in_=logit_scale.unsqueeze(0))
             if i == 4:
                 load_scales("k")
             load_words(*piece)
+            if i == 0:
+                load_scales("q")
+                load_x("k")
 
         ident_bf = keep.tile([P, P], BF16, name="ident_bf")
         nc.vector.tensor_copy(out=ident_bf[:], in_=ident[:])
@@ -130,12 +134,13 @@ def tile_contraattention_w_kernel(
 
         xc = {}
         xp = {}
-        for s in sides:
+
+        def prepare(s, pool, tags):
             xw = x_sb[s][:].bitcast(F32)
             xg = keep.tile([P, KG, P, 4], BF16, name="xg_" + s, align_bytes=64)
             xgw = xg[:].bitcast(F32)
             for h in range(2):
-                xt = psw.tile([P, 2, 2, P], F32, name="xt_%s_%d" % (s, h), tag="work")
+                xt = pool.tile([P, 2, 2, P], F32, name="xt_%s_%d" % (s, h), tag=tags[h])
                 for gl in range(2):
                     g = 2 * h + gl
                     for u in range(2):
@@ -152,15 +157,7 @@ def tile_contraattention_w_kernel(
                 out=xc[s][:].bitcast(FP8X4), scales=xp[s][:], in_=xg[:].rearrange("p g w t -> p (g w t)")
             )
 
-        bt = psk.tile([P, P], BF16, name="bt")
-        nc.tensor.transpose(bt[:], bstage[:], ident_bf[:])
-        bias = keep.tile([P, 32], F32, name="bias")
-        nc.vector.tensor_copy(out=bias[:], in_=bt[:, 0:32])
-
-        fin = psk.tile([P, 64], F32, name="fin")
-        nc.tensor.matmul(out=fin[:, 48:64], lhsT=spread[:], rhs=bstage[:, 0:16], start=True, stop=True)
-        els = keep.tile([P, 1], F32, name="els")
-        nc.scalar.activation(out=els[:], in_=fin[:, 48 + LTOK : 49 + LTOK], func=ACT.Exp)
+        prepare("q", psw, ("work", "work"))
 
         w1 = keep.tile([P, 1], F32, name="w1")
         w2 = keep.tile([P, 1], F32, name="w2")
@@ -221,23 +218,29 @@ def tile_contraattention_w_kernel(
                 in_=fg[s][:, grp, :, :].rearrange("p w t -> p (w t)"),
             )
 
-        def finish(s, grp):
+        def add_bias(s, grp):
             nc.vector.tensor_tensor(
                 out=fg[s][:, grp, :, :],
                 in0=banks[(s, grp)][:].rearrange("p t w -> p w t"),
                 in1=bias_of(s, grp),
                 op=ALU.add,
             )
-            quantise(s, grp)
 
-        lg = psk.tile([P, P], F32, name="lg")
-        lgt = psk.tile([P, P], F32, name="lgt")
+        def finish(s, *grps):
+            for grp in grps:
+                add_bias(s, grp)
+            for grp in grps:
+                quantise(s, grp)
+
+        acc = {}
 
         def logits(grp):
             cols = slice(grp * P, (grp + 1) * P)
-            for acc, a, b in ((lg, "q", "k"), (lgt, "k", "q")):
+            for nm, a, b in (("lg", "q", "k"), ("lgt", "k", "q")):
+                if grp == 0:
+                    acc[nm] = psk.tile([P, P], F32, name=nm, tag=nm)
                 nc.tensor.matmul_mx(
-                    out=acc[:],
+                    out=acc[nm][:],
                     lhsT=fc[a][:, cols].bitcast(FP8X4),
                     lhsT_scale=fp[a][:, cols],
                     rhs=fc[b][:, cols].bitcast(FP8X4),
@@ -246,28 +249,43 @@ def tile_contraattention_w_kernel(
                     stop=(grp == FG - 1),
                 )
 
+        bt = psk.tile([P, P], BF16, name="bt")
+        bias = keep.tile([P, 32], F32, name="bias")
+        fin = psk.tile([P, 64], F32, name="fin")
+        els = keep.tile([P, 1], F32, name="els")
+
+        def spread_bias():
+            nc.tensor.transpose(bt[:], bstage[:], ident_bf[:])
+            nc.vector.tensor_copy(out=bias[:], in_=bt[:, 0:32])
+
         for i, piece in enumerate(PIECES):
             passes(*piece)
-            if i == 3:
-                for grp in range(FG):
-                    finish("q", grp)
-            if i == 7:
-                finish("k", 0)
-                finish("k", 1)
+            if i == 0:
+                prepare("k", psk, ("lg", "lgt"))
+            if i == 1:
+                spread_bias()
+                finish("q", 0, 1)
+            if i == 2:
+                nc.tensor.matmul(out=fin[:, 48:64], lhsT=spread[:], rhs=mstage[:], start=True, stop=True)
+                nc.scalar.activation(out=els[:], in_=fin[:, 48 + LTOK : 49 + LTOK], func=ACT.Exp)
                 sum_weights()
+            if i == 3:
+                finish("q", 2, 3)
+            if i == 7:
+                finish("k", 0, 1)
             if i == 9:
+                finish("k", 2)
                 logits(0)
                 logits(1)
-            if i == 10:
-                finish("k", 2)
+            if i == 11:
+                logits(2)
         finish("k", 3)
-        logits(2)
         logits(3)
 
         r1 = keep.tile([P, NSEQ], F32, name="r1")
         r2 = keep.tile([P, NSEQ], F32, name="r2")
-        nc.vector.tensor_reduce(out=r1[:], in_=lg[:].rearrange("p (b m) -> p b m", m=LTOK), axis=AX.X, op=ALU.max)
-        nc.vector.tensor_reduce(out=r2[:], in_=lgt[:].rearrange("p (a l) -> p a l", l=LTOK), axis=AX.X, op=ALU.max)
+        nc.vector.tensor_reduce(out=r1[:], in_=acc["lg"][:].rearrange("p (b m) -> p b m", m=LTOK), axis=AX.X, op=ALU.max)
+        nc.vector.tensor_reduce(out=r2[:], in_=acc["lgt"][:].rearrange("p (a l) -> p a l", l=LTOK), axis=AX.X, op=ALU.max)
         hi1 = gram["1h"][:, 0:16]
         hi2 = gram["2h"][:, 32:48]
         nc.vector.tensor_scalar(out=hi1, in0=r1[:], scalar1=w1[:, 0:1], scalar2=None, op0=ALU.mult)

@@ -71,8 +71,12 @@ def tile_contraattention_w_kernel(
 
         bstage = keep.tile([P, P], BF16, name="bstage")
         nc.gpsimd.memset(bstage[:], 0.0)
+        mstage = keep.tile([P, NSEQ], BF16, name="mstage")
+        nc.gpsimd.memset(mstage[:], 0.0)
         for wi, s in enumerate(sides):
             nc.scalar.dma_start(out=bstage[16 * wi : 16 * wi + 16, :], in_=b_dram[s].rearrange("(c p) -> c p", p=P))
+        nc.scalar.dma_start(out=mstage[32:48, 0:LTOK], in_=attention_mask)
+        nc.scalar.dma_start(out=mstage[64:65, LTOK : LTOK + 1], in_=logit_scale.unsqueeze(0))
 
         ident = keep.tile([P, P], F32, name="ident")
         make_identity(nc, ident[:])
@@ -83,10 +87,6 @@ def tile_contraattention_w_kernel(
         for nm in ("1h", "1l", "2h", "2l"):
             gram[nm] = keep.tile([P, P], BF16, name="gram_" + nm)
             nc.gpsimd.memset(gram[nm][:], 0.0)
-        mstage = keep.tile([P, NSEQ], BF16, name="mstage")
-        nc.gpsimd.memset(mstage[:], 0.0)
-        nc.gpsimd.dma_start(out=mstage[32:48, 0:LTOK], in_=attention_mask)
-        nc.gpsimd.dma_start(out=mstage[64:65, LTOK : LTOK + 1], in_=logit_scale.unsqueeze(0))
 
         x_sb = {}
         w_sb = {}

@@ -23,17 +23,17 @@ FG = D // 512
 FLOPS = 2 * 2 * P * DIN * D + 2 * P * P * D
 
 PIECES = (
-    ("q", 0, 1024, 0, 2),
-    ("q", 0, 1024, 2, 4),
-    ("q", 1024, 2048, 0, 2),
-    ("q", 1024, 2048, 2, 4),
+    ("q", 0, 2048, 0, 1),
+    ("q", 0, 2048, 1, 2),
+    ("q", 0, 2048, 2, 3),
+    ("q", 0, 2048, 3, 4),
     ("k", 0, 1024, 0, 1),
     ("k", 0, 1024, 1, 2),
     ("k", 0, 1024, 2, 3),
     ("k", 0, 1024, 3, 4),
-    ("k", 1024, 1536, 0, 2),
+    ("k", 1024, 2048, 0, 1),
+    ("k", 1024, 2048, 1, 2),
     ("k", 1024, 1536, 2, 4),
-    ("k", 1536, 2048, 0, 2),
     ("k", 1536, 2048, 2, 3),
     ("k", 1536, 2048, 3, 4),
 )
@@ -73,10 +73,6 @@ def tile_contraattention_w_kernel(
         nc.gpsimd.memset(bstage[:], 0.0)
         mstage = keep.tile([P, NSEQ], BF16, name="mstage")
         nc.gpsimd.memset(mstage[:], 0.0)
-        for wi, s in enumerate(sides):
-            nc.scalar.dma_start(out=bstage[16 * wi : 16 * wi + 16, :], in_=b_dram[s].rearrange("(c p) -> c p", p=P))
-        nc.scalar.dma_start(out=mstage[32:48, 0:LTOK], in_=attention_mask)
-        nc.scalar.dma_start(out=mstage[64:65, LTOK : LTOK + 1], in_=logit_scale.unsqueeze(0))
 
         ident = keep.tile([P, P], F32, name="ident")
         make_identity(nc, ident[:])
@@ -119,6 +115,14 @@ def tile_contraattention_w_kernel(
             if i == 0:
                 load_scales("q")
                 load_x("k")
+            if i == 1:
+                for wi, s in enumerate(sides):
+                    nc.sync.dma_start(
+                        out=bstage[16 * wi : 16 * wi + 16, :], in_=b_dram[s].rearrange("(c p) -> c p", p=P)
+                    )
+            if i == 7:
+                nc.sync.dma_start(out=mstage[32:48, 0:LTOK], in_=attention_mask)
+                nc.sync.dma_start(out=mstage[64:65, LTOK : LTOK + 1], in_=logit_scale.unsqueeze(0))
 
         ident_bf = keep.tile([P, P], BF16, name="ident_bf")
         nc.vector.tensor_copy(out=ident_bf[:], in_=ident[:])
@@ -158,6 +162,10 @@ def tile_contraattention_w_kernel(
             )
 
         prepare("q", psw, ("work", "work"))
+        for nm in ("1h", "1l"):
+            nc.vector.tensor_copy(out=gram[nm][:, 32:48], in_=blk[:])
+        for nm in ("2h", "2l"):
+            nc.vector.tensor_copy(out=gram[nm][:, 0:16], in_=blk[:])
 
         w1 = keep.tile([P, 1], F32, name="w1")
         w2 = keep.tile([P, 1], F32, name="w2")
@@ -171,10 +179,6 @@ def tile_contraattention_w_kernel(
                 out=w1[:], in0=rec[:], scalar1=els[:, 0:1], scalar2=0.5, op0=ALU.mult, op1=ALU.mult
             )
             nc.vector.tensor_scalar(out=w2[:], in0=els[:], scalar1=0.5 / LTOK, scalar2=None, op0=ALU.mult)
-            for nm in ("1h", "1l"):
-                nc.vector.tensor_copy(out=gram[nm][:, 32:48], in_=blk[:])
-            for nm in ("2h", "2l"):
-                nc.vector.tensor_copy(out=gram[nm][:, 0:16], in_=blk[:])
 
         fg = {}
         fc = {}
@@ -262,24 +266,22 @@ def tile_contraattention_w_kernel(
             passes(*piece)
             if i == 0:
                 prepare("k", psk, ("lg", "lgt"))
-            if i == 1:
+            if i == 3:
                 spread_bias()
                 finish("q", 0, 1)
-            if i == 2:
-                nc.tensor.matmul(out=fin[:, 48:64], lhsT=spread[:], rhs=mstage[:], start=True, stop=True)
-                nc.scalar.activation(out=els[:], in_=fin[:, 48 + LTOK : 49 + LTOK], func=ACT.Exp)
-                sum_weights()
-            if i == 3:
                 finish("q", 2, 3)
             if i == 7:
                 finish("k", 0, 1)
+                nc.tensor.matmul(out=fin[:, 48:64], lhsT=spread[:], rhs=mstage[:], start=True, stop=True)
+                nc.scalar.activation(out=els[:], in_=fin[:, 48 + LTOK : 49 + LTOK], func=ACT.Exp)
+                sum_weights()
             if i == 9:
-                finish("k", 2)
                 logits(0)
                 logits(1)
-            if i == 11:
-                logits(2)
+            if i == 10:
+                finish("k", 2)
         finish("k", 3)
+        logits(2)
         logits(3)
 
         r1 = keep.tile([P, NSEQ], F32, name="r1")

@@ -66,7 +66,7 @@ def tile_contraattention_w_kernel(
         psk = ctx.enter_context(tc.psum_pool(name="psk", bufs=1))
         ctx.enter_context(tc.manual_schedule())
 
-        planes = keep.tile([P, 2, D], U8, name="planes", align_bytes=64)
+        planes = keep.tile([P, 2, D], U8, name="planes", align_bytes=256)
         nc.vector.memset(planes[:].rearrange("p w n -> p (w n)").bitcast(I32), 0)
 
         bstage = keep.tile([P, P], BF16, name="bstage")
@@ -88,7 +88,7 @@ def tile_contraattention_w_kernel(
         w_sb = {}
 
         def load_x(s):
-            x_sb[s] = keep.tile([P, DIN], BF16, name="x_" + s)
+            x_sb[s] = keep.tile([P, DIN], BF16, name="x_" + s, align_bytes=256)
             nc.sync.dma_start(out=x_sb[s][:], in_=x_dram[s].rearrange("a l d -> (a l) d"))
 
         def load_scales(s):
@@ -101,7 +101,7 @@ def tile_contraattention_w_kernel(
 
         def load_words(s, n0, n1, g0, g1):
             view = w_dram[s].rearrange("g p n t -> p g (n t)").bitcast(I32)
-            wt = keep.tile([P, g1 - g0, n1 - n0], U32, name="w_%s_%d_%d" % (s, n0, g0), align_bytes=64)
+            wt = keep.tile([P, g1 - g0, n1 - n0], U32, name="w_%s_%d_%d" % (s, n0, g0), align_bytes=256)
             nc.sync.dma_start(out=wt[:].bitcast(I32), in_=view[:, g0:g1, n0:n1])
             for c in range(n0 // P, n1 // P):
                 for g in range(g0, g1):
@@ -141,7 +141,7 @@ def tile_contraattention_w_kernel(
 
         def prepare(s, pool, tags):
             xw = x_sb[s][:].bitcast(F32)
-            xg = keep.tile([P, KG, P, 4], BF16, name="xg_" + s, align_bytes=64)
+            xg = keep.tile([P, KG, P, 4], BF16, name="xg_" + s, align_bytes=256)
             xgw = xg[:].bitcast(F32)
             for h in range(2):
                 xt = pool.tile([P, 2, 2, P], F32, name="xt_%s_%d" % (s, h), tag=tags[h])
@@ -155,8 +155,8 @@ def tile_contraattention_w_kernel(
                     nc.vector.tensor_copy(out=dst, in_=src)
                 else:
                     nc.scalar.copy(out=dst, in_=src)
-            xc[s] = keep.tile([P, KG * P], U32, name="xc_" + s, align_bytes=64)
-            xp[s] = keep.tile([P, KG * P], U8, name="xp_" + s, align_bytes=64)
+            xc[s] = keep.tile([P, KG * P], U32, name="xc_" + s, align_bytes=256)
+            xp[s] = keep.tile([P, KG * P], U8, name="xp_" + s, align_bytes=256)
             nc.vector.quantize_mx(
                 out=xc[s][:].bitcast(FP8X4), scales=xp[s][:], in_=xg[:].rearrange("p g w t -> p (g w t)")
             )
@@ -184,9 +184,9 @@ def tile_contraattention_w_kernel(
         fc = {}
         fp = {}
         for s in sides:
-            fg[s] = keep.tile([P, FG, P, 4], BF16, name="fg_" + s, align_bytes=64)
-            fc[s] = keep.tile([P, FG * P], U32, name="fc_" + s, align_bytes=64)
-            fp[s] = keep.tile([P, FG * P], U8, name="fp_" + s, align_bytes=64)
+            fg[s] = keep.tile([P, FG, P, 4], BF16, name="fg_" + s, align_bytes=256)
+            fc[s] = keep.tile([P, FG * P], U32, name="fc_" + s, align_bytes=256)
+            fp[s] = keep.tile([P, FG * P], U8, name="fp_" + s, align_bytes=256)
 
         banks = {}
         done = {}

@@ -33,8 +33,8 @@ PIECES = (
     ("k", 0, 1024, 3, 4),
     ("k", 1024, 2048, 0, 1),
     ("k", 1024, 2048, 1, 2),
-    ("k", 1024, 1536, 2, 4),
-    ("k", 1536, 2048, 2, 3),
+    ("k", 1024, 2048, 2, 3),
+    ("k", 1024, 1536, 3, 4),
     ("k", 1536, 2048, 3, 4),
 )
 
@@ -120,7 +120,6 @@ def tile_contraattention_w_kernel(
                     nc.sync.dma_start(
                         out=bstage[16 * wi : 16 * wi + 16, :], in_=b_dram[s].rearrange("(c p) -> c p", p=P)
                     )
-            if i == 7:
                 nc.sync.dma_start(out=mstage[32:48, 0:LTOK], in_=attention_mask)
                 nc.sync.dma_start(out=mstage[64:65, LTOK : LTOK + 1], in_=logit_scale.unsqueeze(0))
 
@@ -266,21 +265,20 @@ def tile_contraattention_w_kernel(
             passes(*piece)
             if i == 0:
                 prepare("k", psk, ("lg", "lgt"))
-            if i == 3:
+            if i == 1:
                 spread_bias()
+                nc.tensor.matmul(out=fin[:, 48:64], lhsT=spread[:], rhs=mstage[:], start=True, stop=True)
+                nc.scalar.activation(out=els[:], in_=fin[:, 48 + LTOK : 49 + LTOK], func=ACT.Exp)
+                sum_weights()
+            if i == 3:
                 finish("q", 0, 1)
                 finish("q", 2, 3)
             if i == 7:
                 finish("k", 0, 1)
-                nc.tensor.matmul(out=fin[:, 48:64], lhsT=spread[:], rhs=mstage[:], start=True, stop=True)
-                nc.scalar.activation(out=els[:], in_=fin[:, 48 + LTOK : 49 + LTOK], func=ACT.Exp)
-                sum_weights()
             if i == 9:
                 logits(0)
                 logits(1)
-            if i == 10:
-                finish("k", 2)
-        finish("k", 3)
+        finish("k", 2, 3)
         logits(2)
         logits(3)
 

@@ -80,8 +80,8 @@ def tile_contraattention_w_kernel(
         nc.gpsimd.memset(spread[:], 0.0)
         nc.gpsimd.memset(spread[64:65, :], 1.0)
         gram = {}
-        for nm in ("1h", "1l", "2h", "2l"):
-            gram[nm] = keep.tile([P, P], BF16, name="gram_" + nm)
+        for nm in ("1", "2"):
+            gram[nm] = keep.tile([P, P], F32, name="gram_" + nm)
             nc.gpsimd.memset(gram[nm][:], 0.0)
 
         x_sb = {}
@@ -161,10 +161,6 @@ def tile_contraattention_w_kernel(
             )
 
         prepare("q", psw, ("work", "work"))
-        for nm in ("1h", "1l"):
-            nc.vector.tensor_copy(out=gram[nm][:, 32:48], in_=blk[:])
-        for nm in ("2h", "2l"):
-            nc.vector.tensor_copy(out=gram[nm][:, 0:16], in_=blk[:])
 
         w1 = keep.tile([P, 1], F32, name="w1")
         w2 = keep.tile([P, 1], F32, name="w2")
@@ -178,6 +174,12 @@ def tile_contraattention_w_kernel(
                 out=w1[:], in0=rec[:], scalar1=els[:, 0:1], scalar2=0.5, op0=ALU.mult, op1=ALU.mult
             )
             nc.vector.tensor_scalar(out=w2[:], in0=els[:], scalar1=0.5 / LTOK, scalar2=None, op0=ALU.mult)
+            nc.vector.tensor_scalar(
+                out=gram["1"][:, 32:48], in0=blk[:], scalar1=w1[:, 0:1], scalar2=None, op0=ALU.mult
+            )
+            nc.vector.tensor_scalar(
+                out=gram["2"][:, 0:16], in0=blk[:], scalar1=w2[:, 0:1], scalar2=None, op0=ALU.mult
+            )
 
         fg = {}
         fc = {}
@@ -252,7 +254,7 @@ def tile_contraattention_w_kernel(
                     stop=(grp == FG - 1),
                 )
 
-        bt = psk.tile([P, P], BF16, name="bt")
+        bt = psk.tile([P, P], BF16, name="bt", tag="bt")
         bias = keep.tile([P, 32], F32, name="bias")
         fin = psk.tile([P, 64], F32, name="fin")
         els = keep.tile([P, 1], F32, name="els")
@@ -260,6 +262,17 @@ def tile_contraattention_w_kernel(
         def spread_bias():
             nc.tensor.transpose(bt[:], bstage[:], ident_bf[:])
             nc.vector.tensor_copy(out=bias[:], in_=bt[:, 0:32])
+
+        def keep_clock(n):
+            idle = psk.tile([P, 512], F32, name="idle", tag="bt")
+            for j in range(n):
+                nc.tensor.matmul(
+                    out=idle[:],
+                    lhsT=spread[:],
+                    rhs=fg["q"][:, 0, :, :].rearrange("p w t -> p (w t)"),
+                    start=True,
+                    stop=True,
+                )
 
         for i, piece in enumerate(PIECES):
             passes(*piece)
@@ -279,25 +292,18 @@ def tile_contraattention_w_kernel(
                 logits(0)
                 logits(1)
         finish("k", 2, 3)
+        keep_clock(3)
         logits(2)
         logits(3)
 
-        r1 = keep.tile([P, NSEQ], F32, name="r1")
-        r2 = keep.tile([P, NSEQ], F32, name="r2")
-        nc.vector.tensor_reduce(out=r1[:], in_=acc["lg"][:].rearrange("p (b m) -> p b m", m=LTOK), axis=AX.X, op=ALU.max)
-        nc.vector.tensor_reduce(out=r2[:], in_=acc["lgt"][:].rearrange("p (a l) -> p a l", l=LTOK), axis=AX.X, op=ALU.max)
-        hi1 = gram["1h"][:, 0:16]
-        hi2 = gram["2h"][:, 32:48]
-        nc.vector.tensor_scalar(out=hi1, in0=r1[:], scalar1=w1[:, 0:1], scalar2=None, op0=ALU.mult)
-        nc.vector.tensor_scalar(out=hi2, in0=r2[:], scalar1=w2[:, 0:1], scalar2=None, op0=ALU.mult)
-        nc.vector.scalar_tensor_tensor(
-            out=gram["1l"][:, 0:16], in0=r1[:], scalar=w1[:, 0:1], in1=hi1, op0=ALU.mult, op1=ALU.subtract
+        nc.vector.tensor_reduce(
+            out=gram["1"][:, 0:16], in_=acc["lg"][:].rearrange("p (b m) -> p b m", m=LTOK), axis=AX.X, op=ALU.max
         )
-        nc.vector.scalar_tensor_tensor(
-            out=gram["2l"][:, 32:48], in0=r2[:], scalar=w2[:, 0:1], in1=hi2, op0=ALU.mult, op1=ALU.subtract
+        nc.vector.tensor_reduce(
+            out=gram["2"][:, 32:48], in_=acc["lgt"][:].rearrange("p (a l) -> p a l", l=LTOK), axis=AX.X, op=ALU.max
         )
-        for i, nm in enumerate(("1h", "2h", "1l", "2l")):
-            nc.tensor.matmul(out=fin[:, 0:48], lhsT=gram[nm][:], rhs=gram[nm][:, 0:48], start=(i == 0), stop=(i == 3))
+        for i, nm in enumerate(("1", "2")):
+            nc.tensor.matmul(out=fin[:, 0:48], lhsT=gram[nm][:], rhs=gram[nm][:, 0:48], start=(i == 0), stop=(i == 1))
         res = keep.tile([P, 48], F32, name="res")
         nc.vector.tensor_copy(out=res[:], in_=fin[:, 0:48])
         nc.sync.dma_start(out=out_0, in_=res[32:48, 0:16])

@@ -66,7 +66,7 @@ def tile_contraattention_w_kernel(
         psk = ctx.enter_context(tc.psum_pool(name="psk", bufs=1))
         ctx.enter_context(tc.manual_schedule())
 
-        planes = keep.tile([P, 2, D], U8, name="planes", align_bytes=256)
+        planes = keep.tile([P, 2, D], U8, name="planes", align_bytes=2048)
         nc.vector.memset(planes[:].rearrange("p w n -> p (w n)").bitcast(I32), 0)
 
         bstage = keep.tile([P, P], BF16, name="bstage")
@@ -88,7 +88,7 @@ def tile_contraattention_w_kernel(
         w_sb = {}
 
         def load_x(s):
-            x_sb[s] = keep.tile([P, DIN], BF16, name="x_" + s, align_bytes=256)
+            x_sb[s] = keep.tile([P, DIN], BF16, name="x_" + s, align_bytes=2048)
             nc.sync.dma_start(out=x_sb[s][:], in_=x_dram[s].rearrange("a l d -> (a l) d"))
 
         def load_scales(s):
@@ -101,7 +101,7 @@ def tile_contraattention_w_kernel(
 
         def load_words(s, n0, n1, g0, g1):
             view = w_dram[s].rearrange("g p n t -> p g (n t)").bitcast(I32)
-            wt = keep.tile([P, g1 - g0, n1 - n0], U32, name="w_%s_%d_%d" % (s, n0, g0), align_bytes=256)
+            wt = keep.tile([P, g1 - g0, n1 - n0], U32, name="w_%s_%d_%d" % (s, n0, g0), align_bytes=2048)
             nc.sync.dma_start(out=wt[:].bitcast(I32), in_=view[:, g0:g1, n0:n1])
             for c in range(n0 // P, n1 // P):
                 for g in range(g0, g1):
@@ -175,7 +175,7 @@ def tile_contraattention_w_kernel(
             )
             nc.vector.tensor_scalar(out=w2[:], in0=els[:], scalar1=0.5 / LTOK, scalar2=None, op0=ALU.mult)
             nc.vector.tensor_scalar(
-                out=gram["1"][:, 32:48], in0=blk[:], scalar1=w1[:, 0:1], scalar2=None, op0=ALU.mult
+                out=gram["1"][:, 16:32], in0=blk[:], scalar1=w1[:, 0:1], scalar2=None, op0=ALU.mult
             )
             nc.vector.tensor_scalar(
                 out=gram["2"][:, 0:16], in0=blk[:], scalar1=w2[:, 0:1], scalar2=None, op0=ALU.mult
@@ -300,11 +300,11 @@ def tile_contraattention_w_kernel(
             out=gram["1"][:, 0:16], in_=acc["lg"][:].rearrange("p (b m) -> p b m", m=LTOK), axis=AX.X, op=ALU.max
         )
         nc.vector.tensor_reduce(
-            out=gram["2"][:, 32:48], in_=acc["lgt"][:].rearrange("p (a l) -> p a l", l=LTOK), axis=AX.X, op=ALU.max
+            out=gram["2"][:, 16:32], in_=acc["lgt"][:].rearrange("p (a l) -> p a l", l=LTOK), axis=AX.X, op=ALU.max
         )
         for i, nm in enumerate(("1", "2")):
-            nc.tensor.matmul(out=fin[:, 0:48], lhsT=gram[nm][:], rhs=gram[nm][:, 0:48], start=(i == 0), stop=(i == 1))
-        res = keep.tile([P, 48], F32, name="res")
-        nc.vector.tensor_copy(out=res[:], in_=fin[:, 0:48])
-        nc.sync.dma_start(out=out_0, in_=res[32:48, 0:16])
-        nc.sync.dma_start(out=out_1, in_=res[0:16, 32:48])
+            nc.tensor.matmul(out=fin[:, 0:32], lhsT=gram[nm][:], rhs=gram[nm][:, 0:32], start=(i == 0), stop=(i == 1))
+        res = keep.tile([P, 32], F32, name="res")
+        nc.vector.tensor_copy(out=res[:], in_=fin[:, 0:32])
+        nc.sync.dma_start(out=out_0, in_=res[16:32, 0:16])
+        nc.sync.dma_start(out=out_1, in_=res[0:16, 16:32])

from contextlib import ExitStack

import concourse.mybir as mybir
from concourse.masks import make_identity

F32 = mybir.dt.float32
BF16 = mybir.dt.bfloat16
I32 = mybir.dt.int32
U32 = mybir.dt.uint32
U8 = mybir.dt.uint8
FP8X4 = mybir.dt.float8_e4m3fn_x4
ALU = mybir.AluOpType
ACT = mybir.ActivationFunctionType
AX = mybir.AxisListType

P = 128
DIN = 2048
D = 2048
NSEQ = 16
LTOK = 8
KG = DIN // 512
FG = D // 512
FLOPS = 2 * 2 * P * DIN * D + 2 * P * P * D

PIECES = (
    ("q", 0, 2048, 0, 1),
    ("q", 0, 2048, 1, 2),
    ("q", 0, 2048, 2, 3),
    ("q", 0, 2048, 3, 4),
    ("k", 0, 1024, 0, 1),
    ("k", 0, 1024, 1, 2),
    ("k", 0, 1024, 2, 3),
    ("k", 0, 1024, 3, 4),
    ("k", 1024, 2048, 0, 1),
    ("k", 1024, 2048, 1, 2),
    ("k", 1024, 2048, 2, 3),
    ("k", 1024, 1536, 3, 4),
    ("k", 1536, 2048, 3, 4),
)


def tile_contraattention_w_kernel(
    tc,
    query_states,
    key_states,
    attention_mask,
    Wq_words,
    Wq_scales,
    bq,
    Wk_words,
    Wk_scales,
    bk,
    logit_scale,
    out_0,
    out_1,
):
    nc = tc.nc
    sides = ("q", "k")
    x_dram = {"q": query_states, "k": key_states}
    w_dram = {"q": Wq_words, "k": Wk_words}
    s_dram = {"q": Wq_scales, "k": Wk_scales}
    b_dram = {"q": bq, "k": bk}
    with ExitStack() as ctx:
        keep = ctx.enter_context(tc.tile_pool(name="keep", bufs=1))
        psw = ctx.enter_context(tc.psum_pool(name="psw", bufs=4))
        psk = ctx.enter_context(tc.psum_pool(name="psk", bufs=1))
        ctx.enter_context(tc.manual_schedule())

        planes = keep.tile([P, 2, D], U8, name="planes", align_bytes=2048)
        nc.vector.memset(planes[:].rearrange("p w n -> p (w n)").bitcast(I32), 0)

        bstage = keep.tile([P, P], BF16, name="bstage")
        nc.gpsimd.memset(bstage[:], 0.0)
        mstage = keep.tile([P, NSEQ], BF16, name="mstage")
        nc.gpsimd.memset(mstage[:], 0.0)

        ident = keep.tile([P, P], F32, name="ident")
        make_identity(nc, ident[:])
        spread = keep.tile([P, P], BF16, name="spread")
        nc.gpsimd.memset(spread[:], 0.0)
        nc.gpsimd.memset(spread[64:65, :], 1.0)
        gram = {}
        for nm in ("1", "2"):
            gram[nm] = keep.tile([P, P], F32, name="gram_" + nm)
            nc.gpsimd.memset(gram[nm][:], 0.0)

        x_sb = {}
        w_sb = {}

        def load_x(s):
            x_sb[s] = keep.tile([P, DIN], BF16, name="x_" + s, align_bytes=2048)
            nc.sync.dma_start(out=x_sb[s][:], in_=x_dram[s].rearrange("a l d -> (a l) d"))

        def load_scales(s):
            wi = sides.index(s)
            for quad in range(4):
                nc.sync.dma_start(
                    out=planes[32 * quad : 32 * quad + 16, wi, :].bitcast(I32),
                    in_=s_dram[s][:, 4 * quad : 4 * quad + 4, :].bitcast(I32),
                )

        def load_words(s, n0, n1, g0, g1):
            view = w_dram[s].rearrange("g p n t -> p g (n t)").bitcast(I32)
            wt = keep.tile([P, g1 - g0, n1 - n0], U32, name="w_%s_%d_%d" % (s, n0, g0), align_bytes=2048)
            nc.sync.dma_start(out=wt[:].bitcast(I32), in_=view[:, g0:g1, n0:n1])
            for c in range(n0 // P, n1 // P):
                for g in range(g0, g1):
                    w_sb[(s, c, g)] = wt[:, g - g0, c * P - n0 : (c + 1) * P - n0]

        load_x("q")
        for i, piece in enumerate(PIECES):
            if i == 4:
                load_scales("k")
            load_words(*piece)
            if i == 0:
                load_scales("q")
                load_x("k")
            if i == 1:
                for wi, s in enumerate(sides):
                    nc.sync.dma_start(
                        out=bstage[16 * wi : 16 * wi + 16, :], in_=b_dram[s].rearrange("(c p) -> c p", p=P)
                    )
                nc.sync.dma_start(out=mstage[32:48, 0:LTOK], in_=attention_mask)
                nc.sync.dma_start(out=mstage[64:65, LTOK : LTOK + 1], in_=logit_scale.unsqueeze(0))

        ident_bf = keep.tile([P, P], BF16, name="ident_bf")
        nc.vector.tensor_copy(out=ident_bf[:], in_=ident[:])
        blk = keep.tile([P, NSEQ], F32, name="blk")
        nc.vector.tensor_reduce(
            out=blk[:], in_=ident[:].rearrange("p (a l) -> p a l", l=LTOK), axis=AX.X, op=ALU.add
        )

        nc.vector.tensor_copy(
            out=spread[32:48, :].rearrange("p (a l) -> p a l", l=LTOK),
            in_=ident[32:48, 32:48].unsqueeze(2).to_broadcast([NSEQ, NSEQ, LTOK]),
        )

        xc = {}
        xp = {}

        def prepare(s, pool, tags):
            xw = x_sb[s][:].bitcast(F32)
            xg = keep.tile([P, KG, P, 4], BF16, name="xg_" + s, align_bytes=256)
            xgw = xg[:].bitcast(F32)
            for h in range(2):
                xt = pool.tile([P, 2, 2, P], F32, name="xt_%s_%d" % (s, h), tag=tags[h])
                for gl in range(2):
                    g = 2 * h + gl
                    for u in range(2):
                        nc.tensor.transpose(xt[:, gl, u, :], xw[:, 256 * g + u : 256 * (g + 1) : 2], ident[:])
                src = xt[:].rearrange("p g u w -> p g w u")
                dst = xgw[:, 2 * h : 2 * h + 2, :, :]
                if h == 0:
                    nc.vector.tensor_copy(out=dst, in_=src)
                else:
                    nc.scalar.copy(out=dst, in_=src)
            xc[s] = keep.tile([P, KG * P], U32, name="xc_" + s, align_bytes=256)
            xp[s] = keep.tile([P, KG * P], U8, name="xp_" + s, align_bytes=256)
            nc.vector.quantize_mx(
                out=xc[s][:].bitcast(FP8X4), scales=xp[s][:], in_=xg[:].rearrange("p g w t -> p (g w t)")
            )

        prepare("q", psw, ("work", "work"))

        w1 = keep.tile([P, 1], F32, name="w1")
        w2 = keep.tile([P, 1], F32, name="w2")

        def sum_weights():
            msum = keep.tile([P, 1], F32, name="msum")
            nc.vector.tensor_reduce(out=msum[:], in_=fin[:, 48 : 48 + LTOK], axis=AX.X, op=ALU.add)
            rec = keep.tile([P, 1], F32, name="rec")
            nc.vector.reciprocal(out=rec[:], in_=msum[:])
            nc.vector.tensor_scalar(
                out=w1[:], in0=rec[:], scalar1=els[:, 0:1], scalar2=0.5, op0=ALU.mult, op1=ALU.mult
            )
            nc.vector.tensor_scalar(out=w2[:], in0=els[:], scalar1=0.5 / LTOK, scalar2=None, op0=ALU.mult)
            nc.vector.tensor_scalar(
                out=gram["1"][:, 16:32], in0=blk[:], scalar1=w1[:, 0:1], scalar2=None, op0=ALU.mult
            )
            nc.vector.tensor_scalar(
                out=gram["2"][:, 0:16], in0=blk[:], scalar1=w2[:, 0:1], scalar2=None, op0=ALU.mult
            )

        fg = {}
        fc = {}
        fp = {}
        for s in sides:
            fg[s] = keep.tile([P, FG, P, 4], BF16, name="fg_" + s, align_bytes=256)
            fc[s] = keep.tile([P, FG * P], U32, name="fc_" + s, align_bytes=256)
            fp[s] = keep.tile([P, FG * P], U8, name="fp_" + s, align_bytes=256)

        banks = {}
        done = {}

        def passes(s, n0, n1, g0, g1):
            wi = sides.index(s)
            for g in range(g0, g1):
                for c in range(n0 // P, n1 // P):
                    grp = c // 4
                    if (s, grp) not in banks:
                        banks[(s, grp)] = psw.tile([P, 4, P], F32, name="ps_%s_%d" % (s, grp), tag="work")
                        done[(s, grp)] = 0
                    nc.tensor.matmul_mx(
                        out=banks[(s, grp)][:, c % 4, :],
                        lhsT=w_sb[(s, c, g)].bitcast(FP8X4),
                        lhsT_scale=planes[4 * g : P, wi, c * P : (c + 1) * P],
                        rhs=xc[s][:, g * P : (g + 1) * P].bitcast(FP8X4),
                        rhs_scale=xp[s][:, g * P : (g + 1) * P],
                        start=(done[(s, grp)] == 0),
                        stop=(done[(s, grp)] == 4 * KG - 1),
                    )
                    done[(s, grp)] = done[(s, grp)] + 1

        def bias_of(s, grp):
            b0 = 16 * sides.index(s) + 4 * grp
            return bias[:, b0 : b0 + 4].unsqueeze(1).to_broadcast([P, P, 4])

        def quantise(s, grp):
            cols = slice(grp * P, (grp + 1) * P)
            nc.vector.quantize_mx(
                out=fc[s][:, cols].bitcast(FP8X4),
                scales=fp[s][:, cols],
                in_=fg[s][:, grp, :, :].rearrange("p w t -> p (w t)"),
            )

        def add_bias(s, grp):
            nc.vector.tensor_tensor(
                out=fg[s][:, grp, :, :],
                in0=banks[(s, grp)][:].rearrange("p t w -> p w t"),
                in1=bias_of(s, grp),
                op=ALU.add,
            )

        def finish(s, *grps):
            for grp in grps:
                add_bias(s, grp)
            for grp in grps:
                quantise(s, grp)

        acc = {}

        def logits(grp):
            cols = slice(grp * P, (grp + 1) * P)
            for nm, a, b in (("lg", "q", "k"), ("lgt", "k", "q")):
                if grp == 0:
                    acc[nm] = psk.tile([P, P], F32, name=nm, tag=nm)
                nc.tensor.matmul_mx(
                    out=acc[nm][:],
                    lhsT=fc[a][:, cols].bitcast(FP8X4),
                    lhsT_scale=fp[a][:, cols],
                    rhs=fc[b][:, cols].bitcast(FP8X4),
                    rhs_scale=fp[b][:, cols],
                    start=(grp == 0),
                    stop=(grp == FG - 1),
                )

        bt = psk.tile([P, P], BF16, name="bt", tag="bt")
        bias = keep.tile([P, 32], F32, name="bias")
        fin = psk.tile([P, 64], F32, name="fin")
        els = keep.tile([P, 1], F32, name="els")

        def spread_bias():
            nc.tensor.transpose(bt[:], bstage[:], ident_bf[:])
            nc.vector.tensor_copy(out=bias[:], in_=bt[:, 0:32])

        def keep_clock(n):
            idle = psk.tile([P, 512], F32, name="idle", tag="bt")
            for j in range(n):
                nc.tensor.matmul(
                    out=idle[:],
                    lhsT=spread[:],
                    rhs=fg["q"][:, 0, :, :].rearrange("p w t -> p (w t)"),
                    start=True,
                    stop=True,
                )

        for i, piece in enumerate(PIECES):
            passes(*piece)
            if i == 0:
                prepare("k", psk, ("lg", "lgt"))
            if i == 1:
                spread_bias()
                nc.tensor.matmul(out=fin[:, 48:64], lhsT=spread[:], rhs=mstage[:], start=True, stop=True)
                nc.scalar.activation(out=els[:], in_=fin[:, 48 + LTOK : 49 + LTOK], func=ACT.Exp)
                sum_weights()
            if i == 3:
                finish("q", 0, 1)
                finish("q", 2, 3)
            if i == 7:
                finish("k", 0, 1)
            if i == 9:
                logits(0)
                logits(1)
        finish("k", 2, 3)
        keep_clock(3)
        logits(2)
        logits(3)

        nc.vector.tensor_reduce(
            out=gram["1"][:, 0:16], in_=acc["lg"][:].rearrange("p (b m) -> p b m", m=LTOK), axis=AX.X, op=ALU.max
        )
        nc.vector.tensor_reduce(
            out=gram["2"][:, 16:32], in_=acc["lgt"][:].rearrange("p (a l) -> p a l", l=LTOK), axis=AX.X, op=ALU.max
        )
        for i, nm in enumerate(("1", "2")):
            nc.tensor.matmul(out=fin[:, 0:32], lhsT=gram[nm][:], rhs=gram[nm][:, 0:32], start=(i == 0), stop=(i == 1))
        res = keep.tile([P, 32], F32, name="res")
        nc.vector.tensor_copy(out=res[:], in_=fin[:, 0:32])
        nc.sync.dma_start(out=out_0, in_=res[16:32, 0:16])
        nc.sync.dma_start(out=out_1, in_=res[0:16, 16:32])
